import numpy as np
import ml_dtypes


def mxq(x, axis, fmt="e4m3"):
    dtype, down = {"e4m3": (ml_dtypes.float8_e4m3fn, 7), "e5m2": (ml_dtypes.float8_e5m2, 14)}[fmt]
    v = np.moveaxis(np.asarray(x, np.float32).astype(ml_dtypes.bfloat16).astype(np.float64), axis, -1)
    blocks = v.reshape(v.shape[:-1] + (-1, 32))
    amax = np.abs(blocks).max(-1, keepdims=True)
    byte = np.maximum(np.where(amax > 0, np.frexp(amax)[1] - 1 + 127, 0) - down, 1)
    scale = np.exp2(byte - 127.0)
    codes = (blocks / scale).astype(np.float32).astype(dtype).astype(np.float64)
    return np.moveaxis((codes * scale).reshape(v.shape), -1, axis)


WIDE = False


def mx_kscale(k):
    if not WIDE:
        return np.ones(k)
    levels = np.array([10, -10, 5, -5, 0])
    a = np.random.permutation(np.resize(levels, k // 512 * 4)).reshape(k // 512, 4)
    idx = np.arange(k)
    return np.exp2(a[idx // 512, idx % 128 // 32])


BF16 = ml_dtypes.bfloat16


def bf(x):
    return np.asarray(x, np.float32).astype(BF16)


def f64(x):
    return np.asarray(x).astype(np.float64)


B, D, E = 32, 1024, 256
S = E // 2


def rope(y):
    n = y.shape[-1]
    inv_freq = 1.0 / (10000.0 ** (np.arange(0.0, n, 2.0) / n))
    freqs = inv_freq * np.arange(y.shape[1], dtype=np.float64)
    sin = np.sin(freqs)[None, :, None]
    cos = np.cos(freqs)[None, :, None]
    y1 = y[..., ::2]
    y2 = y[..., 1::2]
    return np.concatenate([y1 * cos - y2 * sin, y1 * sin + y2 * cos], axis=-1)


def setup_inputs():
    s = mx_kscale(D)
    return {"x": bf(np.random.standard_normal((B, S, D)) * s),
            "Wk": bf(np.random.standard_normal((E, D)) / np.sqrt(D) / s[None, :]),
            "bk": bf(np.random.standard_normal(E) * 0.3),
            "Wq": bf(np.random.standard_normal((E, D)) / np.sqrt(D) / s[None, :]),
            "bq": bf(np.random.standard_normal(E) * 0.3),
            "Wv": bf(np.random.standard_normal((E, D)) / np.sqrt(D) / s[None, :]),
            "bv": bf(np.random.standard_normal(E) * 0.3)}


def reference(x, Wk, bk, Wq, bq, Wv, bv):
    xq = mxq(f64(x), 2, "e4m3")
    K = rope((xq @ mxq(f64(Wk), 1, "e4m3").T) + f64(bk))
    Q = rope((xq @ mxq(f64(Wq), 1, "e4m3").T) + f64(bq))
    V = (xq @ mxq(f64(Wv), 1, "e4m3").T) + f64(bv)
    return (K, Q, V)

@@ -1,0 +1,276 @@
+import math
+from contextlib import ExitStack
+
+import concourse.mybir as mybir
+from concourse.masks import make_identity
+
+FLOPS = 2 * 4096 * 1024 * 768
+
+F32 = mybir.dt.float32
+BF16 = mybir.dt.bfloat16
+I32 = mybir.dt.int32
+U32 = mybir.dt.uint32
+U8 = mybir.dt.uint8
+FP8X4 = mybir.dt.float8_e4m3fn_x4
+ALU = mybir.AluOpType
+ACT = mybir.ActivationFunctionType
+
+P = 128
+D = 1024
+E = 256
+TOKENS = 4096
+NT = 4
+GROUPS = TOKENS // (P * NT)
+PAIRS = TOKENS // (2 * P)
+LOOK = 2
+POOL_TILES = ()
+
+
+def tile_attention_t_kernel(tc, x, Wk, bk, Wq, bq, Wv, bv, out_0, out_1, out_2):
+    nc = tc.nc
+    with ExitStack() as ctx:
+        ctx.enter_context(tc.manual_schedule())
+        const = ctx.enter_context(tc.tile_pool(name="const", bufs=1))
+        xpool = ctx.enter_context(tc.tile_pool(name="xpool", bufs=1))
+        gpool = ctx.enter_context(tc.tile_pool(name="gpool", bufs=2))
+        cpool = ctx.enter_context(tc.tile_pool(name="cpool", bufs=LOOK + 2))
+        tpool = ctx.enter_context(tc.tile_pool(name="tpool", bufs=4))
+        opool = ctx.enter_context(tc.tile_pool(name="opool", bufs=3))
+        ps_t = ctx.enter_context(tc.psum_pool(name="ps_t", bufs=2))
+        ps_kq = ctx.enter_context(tc.psum_pool(name="ps_kq", bufs=4))
+        ps_v = ctx.enter_context(tc.psum_pool(name="ps_v", bufs=2))
+
+        xv = x.flatten_outer_dims().rearrange("(g q t) d -> g q (t d)", q=P, t=NT)
+        outs = [
+            o.flatten_outer_dims().rearrange("(g q t) e -> g q (t e)", q=P, t=NT)
+            for o in (out_0, out_1, out_2)
+        ]
+
+        brow = const.tile([P, 3 * E], BF16, name="brow")
+        ones = const.tile([P, P], BF16, name="ones")
+        nc.vector.memset(brow[:], 0.0)
+        nc.vector.memset(ones[:], 1.0)
+        for n, b in enumerate((bk, bq, bv)):
+            nc.scalar.dma_start(out=brow[0:1, n * E:(n + 1) * E], in_=b.rearrange("(o e) -> o e", o=1))
+
+        wraw = []
+        for n, w in enumerate((Wk, Wq, Wv)):
+            wraw.append(const.tile([P, 2 * D], BF16, name="wraw%d" % n))
+        xs = []
+        for g in range(GROUPS):
+            xs.append(xpool.tile([P, NT * D], BF16, name="xs%d" % g))
+        nc.sync.dma_start(out=wraw[0][:], in_=Wk.rearrange("(j h) d -> j (h d)", h=2))
+        nc.sync.dma_start(out=wraw[1][:], in_=Wq.rearrange("(j h) d -> j (h d)", h=2))
+        nc.sync.dma_start(out=xs[0][:], in_=xv[0])
+        nc.sync.dma_start(
+            out=wraw[2][:].rearrange("j (h d) -> j h d", h=2),
+            in_=Wv.rearrange("(h j) d -> j h d", h=2),
+        )
+        for g in range(1, GROUPS):
+            nc.sync.dma_start(out=xs[g][:], in_=xv[g])
+
+        pos_i = const.tile([P, NT], I32, name="pos_i")
+        nc.gpsimd.iota(pos_i[:], pattern=[[1, NT]], base=0, channel_multiplier=NT)
+        ident = const.tile([P, P], F32, name="ident")
+        make_identity(nc, ident[:])
+
+        pos_m = const.tile([P, NT], I32, name="pos_m")
+        nc.vector.tensor_single_scalar(out=pos_m[:], in_=pos_i[:], scalar=127, op=ALU.bitwise_and)
+        pos_f = const.tile([P, NT], F32, name="pos_f")
+        nc.vector.tensor_copy(out=pos_f[:], in_=pos_m[:])
+        decay = const.tile([P, NT], F32, name="decay")
+        nc.scalar.activation(out=decay[:], in_=pos_f[:], func=ACT.Exp, scale=-math.log(10000.0) / 128.0)
+        theta = const.tile([P, NT], F32, name="theta")
+        nc.vector.tensor_tensor(out=theta[:], in0=pos_f[:], in1=decay[:], op=ALU.mult)
+        s_half = const.tile([P, NT], F32, name="s_half")
+        s_quart = const.tile([P, NT], F32, name="s_quart")
+        nc.scalar.activation(out=s_half[:], in_=theta[:], func=ACT.Sin, scale=0.5)
+        nc.scalar.activation(out=s_quart[:], in_=theta[:], func=ACT.Sin, scale=0.25)
+
+        bkq_ps = ps_kq.tile([P, 2 * E], F32, name="bkq_ps", tag="kq")
+        bv_ps = ps_v.tile([P, 2, E], F32, name="bv_ps", tag="v")
+        nc.tensor.matmul(out=bkq_ps[:], lhsT=ones[:], rhs=brow[:, 0:2 * E], start=True, stop=True)
+        nc.tensor.matmul(out=bv_ps[:, 0, :], lhsT=ones[:], rhs=brow[:, 2 * E:3 * E], start=True, stop=True)
+        b_eo = const.tile([P, 2 * E], F32, name="b_eo")
+        b_sw = const.tile([P, 2 * E], F32, name="b_sw")
+        b_v = const.tile([P, E], F32, name="b_v")
+        bkq_view = bkq_ps[:].rearrange("p (w j h) -> p h w j", w=2, h=2)
+        nc.scalar.copy(out=b_eo[:].rearrange("p (h w j) -> p h w j", h=2, w=2), in_=bkq_view)
+        nc.scalar.copy(out=b_sw[:, 0:E].rearrange("p (w j) -> p w j", w=2), in_=bkq_view[:, 1])
+        nc.scalar.mul(out=b_sw[:, E:2 * E].rearrange("p (w j) -> p w j", w=2), in_=bkq_view[:, 0], mul=-1.0)
+        nc.scalar.copy(out=b_v[:], in_=bv_ps[:, 0, :])
+
+        wgrp = const.tile([P, 2 * 6 * 4 * P], BF16, name="wgrp", align_bytes=64)
+        wcod = const.tile([P, 2, 6 * P], U32, name="wcod", align_bytes=64)
+        wscl = const.tile([P, 2, 6 * P], U8, name="wscl", align_bytes=64)
+        wgrp_w = wgrp[:].bitcast(F32).rearrange("p (g c r u) -> p g c r u", g=2, c=6, u=2)
+
+        def transposes(words):
+            tb = ps_t.tile([P, 4, P], F32, name="tb", tag="t")
+            for c in range(4):
+                nc.tensor.transpose(tb[:, c, :], words[:, c * P:(c + 1) * P], ident[:])
+            return tb[:].rearrange("p (g u) q -> p g q u", u=2)
+
+        def weight_tile(col, raw, half, on_vector):
+            src = transposes(raw[:].bitcast(F32)[:, half * (D // 2):(half + 1) * (D // 2)])
+            if on_vector:
+                nc.vector.tensor_copy(out=wgrp_w[:, :, col], in_=src)
+            else:
+                nc.scalar.copy(out=wgrp_w[:, :, col], in_=src)
+
+        def weight_quant(lo, hi):
+            for g in range(2):
+                nc.vector.quantize_mx(
+                    out=wcod[:, g, lo * P:hi * P].bitcast(FP8X4),
+                    scales=wscl[:, g, lo * P:hi * P],
+                    in_=wgrp[:, (g * 6 + lo) * 4 * P:(g * 6 + hi) * 4 * P],
+                )
+
+        grouped = {}
+        codes = {}
+
+        def front_a(i, second_on_vector):
+            grp = gpool.tile([P, 2 * D], BF16, name="grp", tag="grp", align_bytes=64)
+            grp_w = grp[:].bitcast(F32).rearrange("p (s g q u) -> p s g q u", s=2, g=2, u=2)
+            for s in range(2):
+                tl = 2 * i + s
+                words = xs[tl // NT][:].bitcast(F32)
+                src = transposes(words[:, (tl % NT) * (D // 2):(tl % NT + 1) * (D // 2)])
+                if s == 1 and second_on_vector:
+                    nc.vector.tensor_copy(out=grp_w[:, s], in_=src)
+                else:
+                    nc.scalar.copy(out=grp_w[:, s], in_=src)
+            grouped[i] = grp
+
+        def front_b(i):
+            cod = cpool.tile([P, 4 * P], U32, name="cod", tag="cod", align_bytes=64)
+            scl = cpool.tile([P, 4 * P], U8, name="scl", tag="scl", align_bytes=64)
+            nc.vector.quantize_mx(out=cod[:].bitcast(FP8X4), scales=scl[:], in_=grouped[i][:])
+            codes[i] = (cod, scl)
+
+        weight_tile(0, wraw[0], 0, False)
+        weight_tile(2, wraw[0], 1, True)
+        weight_tile(1, wraw[1], 0, False)
+        weight_tile(3, wraw[1], 1, True)
+
+        sq_q = const.tile([P, NT], F32, name="sq_q")
+        c_half = const.tile([P, NT], F32, name="c_half")
+        sin_t = const.tile([P, NT], F32, name="sin_t")
+        sq_h = const.tile([P, NT], F32, name="sq_h")
+        cos_t = const.tile([P, NT], F32, name="cos_t")
+        nc.vector.tensor_tensor(out=sq_q[:], in0=s_quart[:], in1=s_quart[:], op=ALU.mult)
+        nc.vector.tensor_tensor(out=sq_h[:], in0=s_half[:], in1=s_half[:], op=ALU.mult)
+        nc.vector.tensor_scalar(out=c_half[:], in0=sq_q[:], scalar1=-2.0, scalar2=1.0, op0=ALU.mult, op1=ALU.add)
+        nc.vector.tensor_scalar(out=cos_t[:], in0=sq_h[:], scalar1=-2.0, scalar2=1.0, op0=ALU.mult, op1=ALU.add)
+        nc.vector.scalar_tensor_tensor(
+            out=sin_t[:], in0=s_half[:], scalar=2.0, in1=c_half[:], op0=ALU.mult, op1=ALU.mult
+        )
+
+        weight_quant(0, 4)
+        front_a(0, True)
+        weight_tile(4, wraw[2], 0, False)
+        weight_tile(5, wraw[2], 1, True)
+        front_b(0)
+        weight_quant(4, 6)
+        front_a(1, True)
+        front_b(1)
+
+        bias_x = const.tile([P, NT, 2 * E], F32, name="bias_x")
+
+        def bias_table(t):
+            tmp = tpool.tile([P, 2 * E], F32, name="tmp", tag="tmp", bufs=2)
+            nc.scalar.activation(out=tmp[:], in_=b_sw[:], func=ACT.Copy, scale=cos_t[:, t:t + 1])
+            nc.vector.scalar_tensor_tensor(
+                out=bias_x[:, t, :], in0=b_eo[:], scalar=sin_t[:, t:t + 1], in1=tmp[:],
+                op0=ALU.mult, op1=ALU.add,
+            )
+
+        def mx_pair(i):
+            cod, scl = codes[i]
+            kq = []
+            for s in range(2):
+                acc = ps_kq.tile([P, 2 * E], F32, name="kq", tag="kq")
+                for g in range(2):
+                    cols = slice((2 * s + g) * P, (2 * s + g + 1) * P)
+                    nc.tensor.matmul_mx(
+                        out=acc[:], lhsT=cod[:, cols].bitcast(FP8X4), lhsT_scale=scl[:, cols],
+                        rhs=wcod[:, g, 0:4 * P].bitcast(FP8X4), rhs_scale=wscl[:, g, 0:4 * P],
+                        start=(g == 0), stop=(g == 1),
+                    )
+                kq.append(acc)
+            vb = ps_v.tile([P, 2, E], F32, name="vb", tag="v")
+            for s in range(2):
+                for g in range(2):
+                    cols = slice((2 * s + g) * P, (2 * s + g + 1) * P)
+                    nc.tensor.matmul_mx(
+                        out=vb[:, s, :], lhsT=cod[:, cols].bitcast(FP8X4), lhsT_scale=scl[:, cols],
+                        rhs=wcod[:, g, 4 * P:6 * P].bitcast(FP8X4), rhs_scale=wscl[:, g, 4 * P:6 * P],
+                        start=(g == 0), stop=(g == 1),
+                    )
+            return kq, vb
+
+        stage = {}
+
+        def halves(ap):
+            return ap.rearrange("p (w j) -> p w j", w=2)
+
+        def back(i, kq, vb):
+            g = (2 * i) // NT
+            if g not in stage:
+                stage[g] = opool.tile([P, 3, NT, E], F32, name="stage", tag="stage")
+            o = stage[g]
+            ts = []
+            cs = []
+            for s in range(2):
+                tl = 2 * i + s
+                t = tl % NT
+                if (tl % 8) in POOL_TILES:
+                    c_sb = tpool.tile([P, 2 * E], F32, name="c_sb", tag="c_sb")
+                    nc.scalar.activation(out=c_sb[:], in_=kq[s][:], func=ACT.Copy, scale=cos_t[:, t:t + 1])
+                    cs.append(c_sb)
+                else:
+                    cs.append(None)
+                t_sb = tpool.tile([P, 2 * E], F32, name="t_sb", tag="t_sb")
+                nc.vector.scalar_tensor_tensor(
+                    out=t_sb[:], in0=kq[s][:], scalar=sin_t[:, t:t + 1], in1=bias_x[:, t, :],
+                    op0=ALU.mult, op1=ALU.add,
+                )
+                ts.append(t_sb)
+            for s in range(2):
+                t = (2 * i + s) % NT
+                out_a = o[:, 0:2, t, 0:P]
+                out_b = o[:, 0:2, t, P:2 * P]
+                if cs[s] is None:
+                    nc.vector.scalar_tensor_tensor(
+                        out=out_a, in0=halves(kq[s][:, 0:E]), scalar=cos_t[:, t:t + 1],
+                        in1=halves(ts[s][:, E:2 * E]), op0=ALU.mult, op1=ALU.subtract,
+                    )
+                    nc.vector.scalar_tensor_tensor(
+                        out=out_b, in0=halves(kq[s][:, E:2 * E]), scalar=cos_t[:, t:t + 1],
+                        in1=halves(ts[s][:, 0:E]), op0=ALU.mult, op1=ALU.add,
+                    )
+                else:
+                    nc.gpsimd.tensor_tensor(
+                        out=out_a, in0=halves(cs[s][:, 0:E]), in1=halves(ts[s][:, E:2 * E]), op=ALU.subtract
+                    )
+                    nc.gpsimd.tensor_tensor(
+                        out=out_b, in0=halves(cs[s][:, E:2 * E]), in1=halves(ts[s][:, 0:E]), op=ALU.add
+                    )
+            t0 = (2 * i) % NT
+            nc.vector.tensor_tensor(
+                out=o[:, 2, t0:t0 + 2, :], in0=vb[:], in1=b_v[:].unsqueeze(1).to_broadcast([P, 2, E]), op=ALU.add
+            )
+            if t0 + 2 == NT:
+                for n in range(3):
+                    nc.sync.dma_start(out=outs[n][g], in_=o[:, n, :, :].rearrange("p t e -> p (t e)"))
+
+        for i in range(PAIRS):
+            if i + LOOK < PAIRS:
+                front_a(i + LOOK, False)
+            kq, vb = mx_pair(i)
+            if 2 * i < NT:
+                bias_table(2 * i)
+                bias_table(2 * i + 1)
+            back(i, kq, vb)
+            if i + LOOK < PAIRS:
+                front_b(i + LOOK)

@@ -23,7 +23,7 @@ NT = 4
 GROUPS = TOKENS // (P * NT)
 PAIRS = TOKENS // (2 * P)
 LOOK = 2
-POOL_TILES = ()
+POOL_TILES = (0, 1, 2, 3, 4, 5, 6, 7)
 
 
 def tile_attention_t_kernel(tc, x, Wk, bk, Wq, bq, Wv, bv, out_0, out_1, out_2):
@@ -47,11 +47,12 @@ def tile_attention_t_kernel(tc, x, Wk, bk, Wq, bq, Wv, bv, out_0, out_1, out_2):
         ]
 
         brow = const.tile([P, 3 * E], BF16, name="brow")
+        bland = const.tile([P, 3 * E], BF16, name="bland")
         ones = const.tile([P, P], BF16, name="ones")
+        for n, b in enumerate((bk, bq, bv)):
+            nc.scalar.dma_start(out=bland[0:1, n * E:(n + 1) * E], in_=b.rearrange("(o e) -> o e", o=1))
         nc.vector.memset(brow[:], 0.0)
         nc.vector.memset(ones[:], 1.0)
-        for n, b in enumerate((bk, bq, bv)):
-            nc.scalar.dma_start(out=brow[0:1, n * E:(n + 1) * E], in_=b.rearrange("(o e) -> o e", o=1))
 
         wraw = []
         for n, w in enumerate((Wk, Wq, Wv)):
@@ -61,11 +62,12 @@ def tile_attention_t_kernel(tc, x, Wk, bk, Wq, bq, Wv, bv, out_0, out_1, out_2):
             xs.append(xpool.tile([P, NT * D], BF16, name="xs%d" % g))
         nc.sync.dma_start(out=wraw[0][:], in_=Wk.rearrange("(j h) d -> j (h d)", h=2))
         nc.sync.dma_start(out=wraw[1][:], in_=Wq.rearrange("(j h) d -> j (h d)", h=2))
-        nc.sync.dma_start(out=xs[0][:], in_=xv[0])
+        nc.sync.dma_start(out=xs[0][:, 0:2 * D], in_=xv[0][:, 0:2 * D])
         nc.sync.dma_start(
             out=wraw[2][:].rearrange("j (h d) -> j h d", h=2),
             in_=Wv.rearrange("(h j) d -> j h d", h=2),
         )
+        nc.sync.dma_start(out=xs[0][:, 2 * D:4 * D], in_=xv[0][:, 2 * D:4 * D])
         for g in range(1, GROUPS):
             nc.sync.dma_start(out=xs[g][:], in_=xv[g])
 
@@ -87,32 +89,20 @@ def tile_attention_t_kernel(tc, x, Wk, bk, Wq, bq, Wv, bv, out_0, out_1, out_2):
         nc.scalar.activation(out=s_half[:], in_=theta[:], func=ACT.Sin, scale=0.5)
         nc.scalar.activation(out=s_quart[:], in_=theta[:], func=ACT.Sin, scale=0.25)
 
-        bkq_ps = ps_kq.tile([P, 2 * E], F32, name="bkq_ps", tag="kq")
-        bv_ps = ps_v.tile([P, 2, E], F32, name="bv_ps", tag="v")
-        nc.tensor.matmul(out=bkq_ps[:], lhsT=ones[:], rhs=brow[:, 0:2 * E], start=True, stop=True)
-        nc.tensor.matmul(out=bv_ps[:, 0, :], lhsT=ones[:], rhs=brow[:, 2 * E:3 * E], start=True, stop=True)
-        b_eo = const.tile([P, 2 * E], F32, name="b_eo")
-        b_sw = const.tile([P, 2 * E], F32, name="b_sw")
-        b_v = const.tile([P, E], F32, name="b_v")
-        bkq_view = bkq_ps[:].rearrange("p (w j h) -> p h w j", w=2, h=2)
-        nc.scalar.copy(out=b_eo[:].rearrange("p (h w j) -> p h w j", h=2, w=2), in_=bkq_view)
-        nc.scalar.copy(out=b_sw[:, 0:E].rearrange("p (w j) -> p w j", w=2), in_=bkq_view[:, 1])
-        nc.scalar.mul(out=b_sw[:, E:2 * E].rearrange("p (w j) -> p w j", w=2), in_=bkq_view[:, 0], mul=-1.0)
-        nc.scalar.copy(out=b_v[:], in_=bv_ps[:, 0, :])
-
         wgrp = const.tile([P, 2 * 6 * 4 * P], BF16, name="wgrp", align_bytes=64)
         wcod = const.tile([P, 2, 6 * P], U32, name="wcod", align_bytes=64)
         wscl = const.tile([P, 2, 6 * P], U8, name="wscl", align_bytes=64)
         wgrp_w = wgrp[:].bitcast(F32).rearrange("p (g c r u) -> p g c r u", g=2, c=6, u=2)
 
-        def transposes(words):
-            tb = ps_t.tile([P, 4, P], F32, name="tb", tag="t")
+        def transposes(words, pool, tag):
+            tb = pool.tile([P, 4, P], F32, name="tb_" + tag, tag=tag)
             for c in range(4):
                 nc.tensor.transpose(tb[:, c, :], words[:, c * P:(c + 1) * P], ident[:])
             return tb[:].rearrange("p (g u) q -> p g q u", u=2)
 
         def weight_tile(col, raw, half, on_vector):
-            src = transposes(raw[:].bitcast(F32)[:, half * (D // 2):(half + 1) * (D // 2)])
+            pool, tag = (ps_kq, "kq") if col < 4 else (ps_v, "v")
+            src = transposes(raw[:].bitcast(F32)[:, half * (D // 2):(half + 1) * (D // 2)], pool, tag)
             if on_vector:
                 nc.vector.tensor_copy(out=wgrp_w[:, :, col], in_=src)
             else:
@@ -135,7 +125,7 @@ def tile_attention_t_kernel(tc, x, Wk, bk, Wq, bq, Wv, bv, out_0, out_1, out_2):
             for s in range(2):
                 tl = 2 * i + s
                 words = xs[tl // NT][:].bitcast(F32)
-                src = transposes(words[:, (tl % NT) * (D // 2):(tl % NT + 1) * (D // 2)])
+                src = transposes(words[:, (tl % NT) * (D // 2):(tl % NT + 1) * (D // 2)], ps_t, "t")
                 if s == 1 and second_on_vector:
                     nc.vector.tensor_copy(out=grp_w[:, s], in_=src)
                 else:
@@ -148,11 +138,21 @@ def tile_attention_t_kernel(tc, x, Wk, bk, Wq, bq, Wv, bv, out_0, out_1, out_2):
             nc.vector.quantize_mx(out=cod[:].bitcast(FP8X4), scales=scl[:], in_=grouped[i][:])
             codes[i] = (cod, scl)
 
-        weight_tile(0, wraw[0], 0, False)
-        weight_tile(2, wraw[0], 1, True)
-        weight_tile(1, wraw[1], 0, False)
-        weight_tile(3, wraw[1], 1, True)
+        nc.vector.tensor_copy(out=brow[0:1, :], in_=bland[0:1, :])
+        bkq_ps = ps_kq.tile([P, 2 * E], F32, name="bkq_ps", tag="kq")
+        bv_ps = ps_v.tile([P, 2, E], F32, name="bv_ps", tag="v")
+        nc.tensor.matmul(out=bkq_ps[:], lhsT=ones[:], rhs=brow[:, 0:2 * E], start=True, stop=True)
+        nc.tensor.matmul(out=bv_ps[:, 0, :], lhsT=ones[:], rhs=brow[:, 2 * E:3 * E], start=True, stop=True)
+        b_eo = const.tile([P, 2 * E], F32, name="b_eo")
+        b_sw = const.tile([P, 2 * E], F32, name="b_sw")
+        b_v = const.tile([P, E], F32, name="b_v")
+        bkq_view = bkq_ps[:].rearrange("p (w j h) -> p h w j", w=2, h=2)
+        nc.scalar.copy(out=b_eo[:].rearrange("p (h w j) -> p h w j", h=2, w=2), in_=bkq_view)
+        nc.scalar.copy(out=b_sw[:, 0:E].rearrange("p (w j) -> p w j", w=2), in_=bkq_view[:, 1])
+        nc.scalar.mul(out=b_sw[:, E:2 * E].rearrange("p (w j) -> p w j", w=2), in_=bkq_view[:, 0], mul=-1.0)
+        nc.scalar.copy(out=b_v[:], in_=bv_ps[:, 0, :])
 
+        weight_tile(0, wraw[0], 0, True)
         sq_q = const.tile([P, NT], F32, name="sq_q")
         c_half = const.tile([P, NT], F32, name="c_half")
         sin_t = const.tile([P, NT], F32, name="sin_t")
@@ -166,11 +166,14 @@ def tile_attention_t_kernel(tc, x, Wk, bk, Wq, bq, Wv, bv, out_0, out_1, out_2):
             out=sin_t[:], in0=s_half[:], scalar=2.0, in1=c_half[:], op0=ALU.mult, op1=ALU.mult
         )
 
+        weight_tile(2, wraw[0], 1, True)
+        weight_tile(1, wraw[1], 0, True)
+        weight_tile(3, wraw[1], 1, True)
         weight_quant(0, 4)
-        front_a(0, True)
-        weight_tile(4, wraw[2], 0, False)
-        weight_tile(5, wraw[2], 1, True)
+        front_a(0, False)
         front_b(0)
+        weight_tile(4, wraw[2], 0, False)
+        weight_tile(5, wraw[2], 1, False)
         weight_quant(4, 6)
         front_a(1, True)
         front_b(1)
@@ -260,17 +263,22 @@ def tile_attention_t_kernel(tc, x, Wk, bk, Wq, bq, Wv, bv, out_0, out_1, out_2):
             nc.vector.tensor_tensor(
                 out=o[:, 2, t0:t0 + 2, :], in0=vb[:], in1=b_v[:].unsqueeze(1).to_broadcast([P, 2, E]), op=ALU.add
             )
-            if t0 + 2 == NT:
+            if g == GROUPS - 1:
+                for n in range(3):
+                    nc.sync.dma_start(
+                        out=outs[n][g][:, t0 * E:(t0 + 2) * E],
+                        in_=o[:, n, t0:t0 + 2, :].rearrange("p t e -> p (t e)"),
+                    )
+            elif t0 + 2 == NT:
                 for n in range(3):
                     nc.sync.dma_start(out=outs[n][g], in_=o[:, n, :, :].rearrange("p t e -> p (t e)"))
 
         for i in range(PAIRS):
-            if i + LOOK < PAIRS:
-                front_a(i + LOOK, False)
             kq, vb = mx_pair(i)
             if 2 * i < NT:
                 bias_table(2 * i)
                 bias_table(2 * i + 1)
             back(i, kq, vb)
             if i + LOOK < PAIRS:
+                front_a(i + LOOK, False)
                 front_b(i + LOOK)

@@ -50,7 +50,7 @@ def tile_attention_t_kernel(tc, x, Wk, bk, Wq, bq, Wv, bv, out_0, out_1, out_2):
         bland = const.tile([P, 3 * E], BF16, name="bland")
         ones = const.tile([P, P], BF16, name="ones")
         for n, b in enumerate((bk, bq, bv)):
-            nc.scalar.dma_start(out=bland[0:1, n * E:(n + 1) * E], in_=b.rearrange("(o e) -> o e", o=1))
+            nc.sync.dma_start(out=bland[0:1, n * E:(n + 1) * E], in_=b.rearrange("(o e) -> o e", o=1))
         nc.vector.memset(brow[:], 0.0)
         nc.vector.memset(ones[:], 1.0)
 
@@ -228,8 +228,8 @@ def tile_attention_t_kernel(tc, x, Wk, bk, Wq, bq, Wv, bv, out_0, out_1, out_2):
                 tl = 2 * i + s
                 t = tl % NT
                 if (tl % 8) in POOL_TILES:
-                    c_sb = tpool.tile([P, 2 * E], F32, name="c_sb", tag="c_sb")
-                    nc.scalar.activation(out=c_sb[:], in_=kq[s][:], func=ACT.Copy, scale=cos_t[:, t:t + 1])
+                    c_sb = tpool.tile([P, E], F32, name="c_sb", tag="c_sb")
+                    nc.scalar.activation(out=c_sb[:], in_=kq[s][:, 0:E], func=ACT.Copy, scale=cos_t[:, t:t + 1])
                     cs.append(c_sb)
                 else:
                     cs.append(None)
@@ -254,10 +254,11 @@ def tile_attention_t_kernel(tc, x, Wk, bk, Wq, bq, Wv, bv, out_0, out_1, out_2):
                     )
                 else:
                     nc.gpsimd.tensor_tensor(
-                        out=out_a, in0=halves(cs[s][:, 0:E]), in1=halves(ts[s][:, E:2 * E]), op=ALU.subtract
+                        out=out_a, in0=halves(cs[s][:]), in1=halves(ts[s][:, E:2 * E]), op=ALU.subtract
                     )
-                    nc.gpsimd.tensor_tensor(
-                        out=out_b, in0=halves(cs[s][:, E:2 * E]), in1=halves(ts[s][:, 0:E]), op=ALU.add
+                    nc.vector.scalar_tensor_tensor(
+                        out=out_b, in0=halves(kq[s][:, E:2 * E]), scalar=cos_t[:, t:t + 1],
+                        in1=halves(ts[s][:, 0:E]), op0=ALU.mult, op1=ALU.add,
                     )
             t0 = (2 * i) % NT
             nc.vector.tensor_tensor(

@@ -19,11 +19,7 @@ P = 128
 D = 1024
 E = 256
 TOKENS = 4096
-NT = 4
-GROUPS = TOKENS // (P * NT)
 PAIRS = TOKENS // (2 * P)
-LOOK = 2
-POOL_TILES = (0, 1, 2, 3, 4, 5, 6, 7)
 
 
 def tile_attention_t_kernel(tc, x, Wk, bk, Wq, bq, Wv, bv, out_0, out_1, out_2):
@@ -33,61 +29,89 @@ def tile_attention_t_kernel(tc, x, Wk, bk, Wq, bq, Wv, bv, out_0, out_1, out_2):
         const = ctx.enter_context(tc.tile_pool(name="const", bufs=1))
         xpool = ctx.enter_context(tc.tile_pool(name="xpool", bufs=1))
         gpool = ctx.enter_context(tc.tile_pool(name="gpool", bufs=2))
-        cpool = ctx.enter_context(tc.tile_pool(name="cpool", bufs=LOOK + 2))
+        cpool = ctx.enter_context(tc.tile_pool(name="cpool", bufs=4))
         tpool = ctx.enter_context(tc.tile_pool(name="tpool", bufs=4))
-        opool = ctx.enter_context(tc.tile_pool(name="opool", bufs=3))
+        opool = ctx.enter_context(tc.tile_pool(name="opool", bufs=4))
         ps_t = ctx.enter_context(tc.psum_pool(name="ps_t", bufs=2))
         ps_kq = ctx.enter_context(tc.psum_pool(name="ps_kq", bufs=4))
         ps_v = ctx.enter_context(tc.psum_pool(name="ps_v", bufs=2))
 
-        xv = x.flatten_outer_dims().rearrange("(g q t) d -> g q (t d)", q=P, t=NT)
+        xv = x.flatten_outer_dims().rearrange("(i q s) d -> i q (s d)", q=P, s=2)
         outs = [
-            o.flatten_outer_dims().rearrange("(g q t) e -> g q (t e)", q=P, t=NT)
+            o.flatten_outer_dims().rearrange("(i q s) e -> i q (s e)", q=P, s=2)
             for o in (out_0, out_1, out_2)
         ]
 
-        brow = const.tile([P, 3 * E], BF16, name="brow")
         bland = const.tile([P, 3 * E], BF16, name="bland")
-        ones = const.tile([P, P], BF16, name="ones")
         for n, b in enumerate((bk, bq, bv)):
             nc.sync.dma_start(out=bland[0:1, n * E:(n + 1) * E], in_=b.rearrange("(o e) -> o e", o=1))
-        nc.vector.memset(brow[:], 0.0)
-        nc.vector.memset(ones[:], 1.0)
-
         wraw = []
-        for n, w in enumerate((Wk, Wq, Wv)):
+        for n in range(3):
             wraw.append(const.tile([P, 2 * D], BF16, name="wraw%d" % n))
         xs = []
-        for g in range(GROUPS):
-            xs.append(xpool.tile([P, NT * D], BF16, name="xs%d" % g))
+        for i in range(PAIRS):
+            xs.append(xpool.tile([P, 2 * D], BF16, name="xs%d" % i))
         nc.sync.dma_start(out=wraw[0][:], in_=Wk.rearrange("(j h) d -> j (h d)", h=2))
         nc.sync.dma_start(out=wraw[1][:], in_=Wq.rearrange("(j h) d -> j (h d)", h=2))
-        nc.sync.dma_start(out=xs[0][:, 0:2 * D], in_=xv[0][:, 0:2 * D])
+        nc.sync.dma_start(out=xs[0][:], in_=xv[0])
         nc.sync.dma_start(
             out=wraw[2][:].rearrange("j (h d) -> j h d", h=2),
             in_=Wv.rearrange("(h j) d -> j h d", h=2),
         )
-        nc.sync.dma_start(out=xs[0][:, 2 * D:4 * D], in_=xv[0][:, 2 * D:4 * D])
-        for g in range(1, GROUPS):
-            nc.sync.dma_start(out=xs[g][:], in_=xv[g])
+        for i in range(1, PAIRS):
+            nc.sync.dma_start(out=xs[i][:], in_=xv[i])
 
-        pos_i = const.tile([P, NT], I32, name="pos_i")
-        nc.gpsimd.iota(pos_i[:], pattern=[[1, NT]], base=0, channel_multiplier=NT)
+        brow = const.tile([P, 3 * E], BF16, name="brow")
+        ones = const.tile([P, P], BF16, name="ones")
+        nc.vector.memset(brow[:], 0.0)
+        nc.vector.memset(ones[:], 1.0)
+        pos_i = const.tile([P, 2], I32, name="pos_i")
+        nc.gpsimd.iota(pos_i[:], pattern=[[1, 2]], base=0, channel_multiplier=2)
         ident = const.tile([P, P], F32, name="ident")
         make_identity(nc, ident[:])
 
-        pos_m = const.tile([P, NT], I32, name="pos_m")
+        pos_m = const.tile([P, 2], I32, name="pos_m")
         nc.vector.tensor_single_scalar(out=pos_m[:], in_=pos_i[:], scalar=127, op=ALU.bitwise_and)
-        pos_f = const.tile([P, NT], F32, name="pos_f")
+        pos_f = const.tile([P, 2], F32, name="pos_f")
         nc.vector.tensor_copy(out=pos_f[:], in_=pos_m[:])
-        decay = const.tile([P, NT], F32, name="decay")
+        decay = const.tile([P, 2], F32, name="decay")
         nc.scalar.activation(out=decay[:], in_=pos_f[:], func=ACT.Exp, scale=-math.log(10000.0) / 128.0)
-        theta = const.tile([P, NT], F32, name="theta")
+        theta = const.tile([P, 2], F32, name="theta")
         nc.vector.tensor_tensor(out=theta[:], in0=pos_f[:], in1=decay[:], op=ALU.mult)
-        s_half = const.tile([P, NT], F32, name="s_half")
-        s_quart = const.tile([P, NT], F32, name="s_quart")
+        s_half = const.tile([P, 2], F32, name="s_half")
+        s_quart = const.tile([P, 2], F32, name="s_quart")
         nc.scalar.activation(out=s_half[:], in_=theta[:], func=ACT.Sin, scale=0.5)
         nc.scalar.activation(out=s_quart[:], in_=theta[:], func=ACT.Sin, scale=0.25)
+
+        nc.vector.tensor_copy(out=brow[0:1, :], in_=bland[0:1, :])
+        bkq_ps = ps_kq.tile([P, 2 * E], F32, name="bkq_ps", tag="kq")
+        bv_ps = ps_v.tile([P, 2, E], F32, name="bv_ps", tag="v")
+        nc.tensor.matmul(out=bkq_ps[:], lhsT=ones[:], rhs=brow[:, 0:2 * E], start=True, stop=True)
+        nc.tensor.matmul(out=bv_ps[:, 0, :], lhsT=ones[:], rhs=brow[:, 2 * E:3 * E], start=True, stop=True)
+        b_eo = const.tile([P, 2 * E], F32, name="b_eo")
+        b_sw = const.tile([P, 2 * E], F32, name="b_sw")
+        b_v = const.tile([P, E], F32, name="b_v")
+        bkq_view = bkq_ps[:].rearrange("p (w j h) -> p h w j", w=2, h=2)
+        nc.scalar.copy(out=b_eo[:].rearrange("p (h w j) -> p h w j", h=2, w=2), in_=bkq_view)
+        nc.vector.tensor_copy(out=b_sw[:, 0:E].rearrange("p (w j) -> p w j", w=2), in_=bkq_view[:, 1])
+        nc.vector.tensor_scalar(
+            out=b_sw[:, E:2 * E].rearrange("p (w j) -> p w j", w=2), in0=bkq_view[:, 0],
+            scalar1=-1.0, scalar2=None, op0=ALU.mult,
+        )
+        nc.scalar.copy(out=b_v[:], in_=bv_ps[:, 0, :])
+
+        sq_q = const.tile([P, 2], F32, name="sq_q")
+        c_half = const.tile([P, 2], F32, name="c_half")
+        sin_t = const.tile([P, 2], F32, name="sin_t")
+        sq_h = const.tile([P, 2], F32, name="sq_h")
+        cos_t = const.tile([P, 2], F32, name="cos_t")
+        nc.vector.tensor_tensor(out=sq_q[:], in0=s_quart[:], in1=s_quart[:], op=ALU.mult)
+        nc.vector.tensor_tensor(out=sq_h[:], in0=s_half[:], in1=s_half[:], op=ALU.mult)
+        nc.vector.tensor_scalar(out=c_half[:], in0=sq_q[:], scalar1=-2.0, scalar2=1.0, op0=ALU.mult, op1=ALU.add)
+        nc.vector.tensor_scalar(out=cos_t[:], in0=sq_h[:], scalar1=-2.0, scalar2=1.0, op0=ALU.mult, op1=ALU.add)
+        nc.vector.scalar_tensor_tensor(
+            out=sin_t[:], in0=s_half[:], scalar=2.0, in1=c_half[:], op0=ALU.mult, op1=ALU.mult
+        )
 
         wgrp = const.tile([P, 2 * 6 * 4 * P], BF16, name="wgrp", align_bytes=64)
         wcod = const.tile([P, 2, 6 * P], U32, name="wcod", align_bytes=64)
@@ -118,18 +142,16 @@ def tile_attention_t_kernel(tc, x, Wk, bk, Wq, bq, Wv, bv, out_0, out_1, out_2):
 
         grouped = {}
         codes = {}
+        banks = {}
+        parts = {}
 
-        def front_a(i, second_on_vector):
+        def front_a(i):
             grp = gpool.tile([P, 2 * D], BF16, name="grp", tag="grp", align_bytes=64)
             grp_w = grp[:].bitcast(F32).rearrange("p (s g q u) -> p s g q u", s=2, g=2, u=2)
+            words = xs[i][:].bitcast(F32)
             for s in range(2):
-                tl = 2 * i + s
-                words = xs[tl // NT][:].bitcast(F32)
-                src = transposes(words[:, (tl % NT) * (D // 2):(tl % NT + 1) * (D // 2)], ps_t, "t")
-                if s == 1 and second_on_vector:
-                    nc.vector.tensor_copy(out=grp_w[:, s], in_=src)
-                else:
-                    nc.scalar.copy(out=grp_w[:, s], in_=src)
+                src = transposes(words[:, s * (D // 2):(s + 1) * (D // 2)], ps_t, "t")
+                nc.scalar.copy(out=grp_w[:, s], in_=src)
             grouped[i] = grp
 
         def front_b(i):
@@ -138,53 +160,13 @@ def tile_attention_t_kernel(tc, x, Wk, bk, Wq, bq, Wv, bv, out_0, out_1, out_2):
             nc.vector.quantize_mx(out=cod[:].bitcast(FP8X4), scales=scl[:], in_=grouped[i][:])
             codes[i] = (cod, scl)
 
-        nc.vector.tensor_copy(out=brow[0:1, :], in_=bland[0:1, :])
-        bkq_ps = ps_kq.tile([P, 2 * E], F32, name="bkq_ps", tag="kq")
-        bv_ps = ps_v.tile([P, 2, E], F32, name="bv_ps", tag="v")
-        nc.tensor.matmul(out=bkq_ps[:], lhsT=ones[:], rhs=brow[:, 0:2 * E], start=True, stop=True)
-        nc.tensor.matmul(out=bv_ps[:, 0, :], lhsT=ones[:], rhs=brow[:, 2 * E:3 * E], start=True, stop=True)
-        b_eo = const.tile([P, 2 * E], F32, name="b_eo")
-        b_sw = const.tile([P, 2 * E], F32, name="b_sw")
-        b_v = const.tile([P, E], F32, name="b_v")
-        bkq_view = bkq_ps[:].rearrange("p (w j h) -> p h w j", w=2, h=2)
-        nc.scalar.copy(out=b_eo[:].rearrange("p (h w j) -> p h w j", h=2, w=2), in_=bkq_view)
-        nc.scalar.copy(out=b_sw[:, 0:E].rearrange("p (w j) -> p w j", w=2), in_=bkq_view[:, 1])
-        nc.scalar.mul(out=b_sw[:, E:2 * E].rearrange("p (w j) -> p w j", w=2), in_=bkq_view[:, 0], mul=-1.0)
-        nc.scalar.copy(out=b_v[:], in_=bv_ps[:, 0, :])
+        bias_x = const.tile([P, 2, 2 * E], F32, name="bias_x")
 
-        weight_tile(0, wraw[0], 0, True)
-        sq_q = const.tile([P, NT], F32, name="sq_q")
-        c_half = const.tile([P, NT], F32, name="c_half")
-        sin_t = const.tile([P, NT], F32, name="sin_t")
-        sq_h = const.tile([P, NT], F32, name="sq_h")
-        cos_t = const.tile([P, NT], F32, name="cos_t")
-        nc.vector.tensor_tensor(out=sq_q[:], in0=s_quart[:], in1=s_quart[:], op=ALU.mult)
-        nc.vector.tensor_tensor(out=sq_h[:], in0=s_half[:], in1=s_half[:], op=ALU.mult)
-        nc.vector.tensor_scalar(out=c_half[:], in0=sq_q[:], scalar1=-2.0, scalar2=1.0, op0=ALU.mult, op1=ALU.add)
-        nc.vector.tensor_scalar(out=cos_t[:], in0=sq_h[:], scalar1=-2.0, scalar2=1.0, op0=ALU.mult, op1=ALU.add)
-        nc.vector.scalar_tensor_tensor(
-            out=sin_t[:], in0=s_half[:], scalar=2.0, in1=c_half[:], op0=ALU.mult, op1=ALU.mult
-        )
-
-        weight_tile(2, wraw[0], 1, True)
-        weight_tile(1, wraw[1], 0, True)
-        weight_tile(3, wraw[1], 1, True)
-        weight_quant(0, 4)
-        front_a(0, False)
-        front_b(0)
-        weight_tile(4, wraw[2], 0, False)
-        weight_tile(5, wraw[2], 1, False)
-        weight_quant(4, 6)
-        front_a(1, True)
-        front_b(1)
-
-        bias_x = const.tile([P, NT, 2 * E], F32, name="bias_x")
-
-        def bias_table(t):
+        def bias_table(s):
             tmp = tpool.tile([P, 2 * E], F32, name="tmp", tag="tmp", bufs=2)
-            nc.scalar.activation(out=tmp[:], in_=b_sw[:], func=ACT.Copy, scale=cos_t[:, t:t + 1])
+            nc.scalar.activation(out=tmp[:], in_=b_sw[:], func=ACT.Copy, scale=cos_t[:, s:s + 1])
             nc.vector.scalar_tensor_tensor(
-                out=bias_x[:, t, :], in0=b_eo[:], scalar=sin_t[:, t:t + 1], in1=tmp[:],
+                out=bias_x[:, s, :], in0=b_eo[:], scalar=sin_t[:, s:s + 1], in1=tmp[:],
                 op0=ALU.mult, op1=ALU.add,
             )
 
@@ -210,76 +192,77 @@ def tile_attention_t_kernel(tc, x, Wk, bk, Wq, bq, Wv, bv, out_0, out_1, out_2):
                         rhs=wcod[:, g, 4 * P:6 * P].bitcast(FP8X4), rhs_scale=wscl[:, g, 4 * P:6 * P],
                         start=(g == 0), stop=(g == 1),
                     )
-            return kq, vb
-
-        stage = {}
+            banks[i] = (kq, vb)
 
         def halves(ap):
             return ap.rearrange("p (w j) -> p w j", w=2)
 
-        def back(i, kq, vb):
-            g = (2 * i) // NT
-            if g not in stage:
-                stage[g] = opool.tile([P, 3, NT, E], F32, name="stage", tag="stage")
-            o = stage[g]
-            ts = []
-            cs = []
+        def back_first(i, pool_adds_b1):
+            kq = banks[i][0]
+            t_pair = tpool.tile([P, 2, 2 * E], F32, name="t_pair", tag="t_pair")
+            c_pair = tpool.tile([P, 2, 2 * E], F32, name="c_pair", tag="c_pair")
             for s in range(2):
-                tl = 2 * i + s
-                t = tl % NT
-                if (tl % 8) in POOL_TILES:
-                    c_sb = tpool.tile([P, E], F32, name="c_sb", tag="c_sb")
-                    nc.scalar.activation(out=c_sb[:], in_=kq[s][:, 0:E], func=ACT.Copy, scale=cos_t[:, t:t + 1])
-                    cs.append(c_sb)
-                else:
-                    cs.append(None)
-                t_sb = tpool.tile([P, 2 * E], F32, name="t_sb", tag="t_sb")
                 nc.vector.scalar_tensor_tensor(
-                    out=t_sb[:], in0=kq[s][:], scalar=sin_t[:, t:t + 1], in1=bias_x[:, t, :],
+                    out=t_pair[:, s, :], in0=kq[s][:], scalar=sin_t[:, s:s + 1], in1=bias_x[:, s, :],
                     op0=ALU.mult, op1=ALU.add,
                 )
-                ts.append(t_sb)
+                width = 2 * E if (s == 1 and pool_adds_b1) else E
+                nc.scalar.activation(
+                    out=c_pair[:, s, 0:width], in_=kq[s][:, 0:width], func=ACT.Copy, scale=cos_t[:, s:s + 1]
+                )
+            parts[i] = (t_pair, c_pair)
+
+        def back_second(i, pool_adds_b1):
+            kq, vb = banks[i]
+            t_pair, c_pair = parts[i]
+            o = opool.tile([P, 3, 2, E], F32, name="stage", tag="stage")
+            nc.gpsimd.tensor_tensor(
+                out=o[:, 0:2, :, 0:P],
+                in0=c_pair[:, :, 0:E].rearrange("p s (w j) -> p w s j", w=2),
+                in1=t_pair[:, :, E:2 * E].rearrange("p s (w j) -> p w s j", w=2),
+                op=ALU.subtract,
+            )
             for s in range(2):
-                t = (2 * i + s) % NT
-                out_a = o[:, 0:2, t, 0:P]
-                out_b = o[:, 0:2, t, P:2 * P]
-                if cs[s] is None:
-                    nc.vector.scalar_tensor_tensor(
-                        out=out_a, in0=halves(kq[s][:, 0:E]), scalar=cos_t[:, t:t + 1],
-                        in1=halves(ts[s][:, E:2 * E]), op0=ALU.mult, op1=ALU.subtract,
-                    )
-                    nc.vector.scalar_tensor_tensor(
-                        out=out_b, in0=halves(kq[s][:, E:2 * E]), scalar=cos_t[:, t:t + 1],
-                        in1=halves(ts[s][:, 0:E]), op0=ALU.mult, op1=ALU.add,
+                if s == 1 and pool_adds_b1:
+                    nc.gpsimd.tensor_tensor(
+                        out=o[:, 0:2, s, P:2 * P], in0=halves(c_pair[:, s, E:2 * E]),
+                        in1=halves(t_pair[:, s, 0:E]), op=ALU.add,
                     )
                 else:
-                    nc.gpsimd.tensor_tensor(
-                        out=out_a, in0=halves(cs[s][:]), in1=halves(ts[s][:, E:2 * E]), op=ALU.subtract
-                    )
                     nc.vector.scalar_tensor_tensor(
-                        out=out_b, in0=halves(kq[s][:, E:2 * E]), scalar=cos_t[:, t:t + 1],
-                        in1=halves(ts[s][:, 0:E]), op0=ALU.mult, op1=ALU.add,
+                        out=o[:, 0:2, s, P:2 * P], in0=halves(kq[s][:, E:2 * E]), scalar=cos_t[:, s:s + 1],
+                        in1=halves(t_pair[:, s, 0:E]), op0=ALU.mult, op1=ALU.add,
                     )
-            t0 = (2 * i) % NT
             nc.vector.tensor_tensor(
-                out=o[:, 2, t0:t0 + 2, :], in0=vb[:], in1=b_v[:].unsqueeze(1).to_broadcast([P, 2, E]), op=ALU.add
+                out=o[:, 2, :, :], in0=vb[:], in1=b_v[:].unsqueeze(1).to_broadcast([P, 2, E]), op=ALU.add
             )
-            if g == GROUPS - 1:
-                for n in range(3):
-                    nc.sync.dma_start(
-                        out=outs[n][g][:, t0 * E:(t0 + 2) * E],
-                        in_=o[:, n, t0:t0 + 2, :].rearrange("p t e -> p (t e)"),
-                    )
-            elif t0 + 2 == NT:
-                for n in range(3):
-                    nc.sync.dma_start(out=outs[n][g], in_=o[:, n, :, :].rearrange("p t e -> p (t e)"))
+            for n in (2, 0, 1):
+                nc.sync.dma_start(out=outs[n][i], in_=o[:, n, :, :].rearrange("p s e -> p (s e)"))
 
+        weight_tile(0, wraw[0], 0, False)
+        weight_tile(2, wraw[0], 1, True)
+        weight_tile(1, wraw[1], 0, False)
+        weight_tile(3, wraw[1], 1, True)
+        weight_quant(0, 4)
+        front_a(0)
+        front_b(0)
+        weight_tile(4, wraw[2], 0, False)
+        weight_tile(5, wraw[2], 1, False)
+        weight_quant(4, 6)
+        front_a(1)
+        front_b(1)
+        mx_pair(0)
+        bias_table(0)
+        bias_table(1)
+        front_a(2)
+        mx_pair(1)
         for i in range(PAIRS):
-            kq, vb = mx_pair(i)
-            if 2 * i < NT:
-                bias_table(2 * i)
-                bias_table(2 * i + 1)
-            back(i, kq, vb)
-            if i + LOOK < PAIRS:
-                front_a(i + LOOK, False)
-                front_b(i + LOOK)
+            pool_adds_b1 = i < PAIRS - 1
+            back_first(i, pool_adds_b1)
+            if i + 2 < PAIRS:
+                front_b(i + 2)
+            back_second(i, pool_adds_b1)
+            if i + 3 < PAIRS:
+                front_a(i + 3)
+            if i + 2 < PAIRS:
+                mx_pair(i + 2)

@@ -144,6 +144,7 @@ def tile_attention_t_kernel(tc, x, Wk, bk, Wq, bq, Wv, bv, out_0, out_1, out_2):
         codes = {}
         banks = {}
         parts = {}
+        cosines = {}
 
         def front_a(i):
             grp = gpool.tile([P, 2 * D], BF16, name="grp", tag="grp", align_bytes=64)
@@ -197,24 +198,33 @@ def tile_attention_t_kernel(tc, x, Wk, bk, Wq, bq, Wv, bv, out_0, out_1, out_2):
         def halves(ap):
             return ap.rearrange("p (w j) -> p w j", w=2)
 
-        def back_first(i, pool_adds_b1):
+        def pool_adds_b1(i):
+            return 0 < i < PAIRS - 1
+
+        def times_cos(i):
+            kq = banks[i][0]
+            c_pair = tpool.tile([P, 2, 2 * E], F32, name="c_pair", tag="c_pair")
+            for s in range(2):
+                width = 2 * E if (s == 1 and pool_adds_b1(i)) else E
+                nc.scalar.activation(
+                    out=c_pair[:, s, 0:width], in_=kq[s][:, 0:width], func=ACT.Copy, scale=cos_t[:, s:s + 1]
+                )
+            cosines[i] = c_pair
+
+        def times_sin(i):
             kq = banks[i][0]
             t_pair = tpool.tile([P, 2, 2 * E], F32, name="t_pair", tag="t_pair")
-            c_pair = tpool.tile([P, 2, 2 * E], F32, name="c_pair", tag="c_pair")
             for s in range(2):
                 nc.vector.scalar_tensor_tensor(
                     out=t_pair[:, s, :], in0=kq[s][:], scalar=sin_t[:, s:s + 1], in1=bias_x[:, s, :],
                     op0=ALU.mult, op1=ALU.add,
                 )
-                width = 2 * E if (s == 1 and pool_adds_b1) else E
-                nc.scalar.activation(
-                    out=c_pair[:, s, 0:width], in_=kq[s][:, 0:width], func=ACT.Copy, scale=cos_t[:, s:s + 1]
-                )
-            parts[i] = (t_pair, c_pair)
+            parts[i] = t_pair
 
-        def back_second(i, pool_adds_b1):
+        def back_second(i):
             kq, vb = banks[i]
-            t_pair, c_pair = parts[i]
+            t_pair = parts[i]
+            c_pair = cosines[i]
             o = opool.tile([P, 3, 2, E], F32, name="stage", tag="stage")
             nc.gpsimd.tensor_tensor(
                 out=o[:, 0:2, :, 0:P],
@@ -223,7 +233,7 @@ def tile_attention_t_kernel(tc, x, Wk, bk, Wq, bq, Wv, bv, out_0, out_1, out_2):
                 op=ALU.subtract,
             )
             for s in range(2):
-                if s == 1 and pool_adds_b1:
+                if s == 1 and pool_adds_b1(i):
                     nc.gpsimd.tensor_tensor(
                         out=o[:, 0:2, s, P:2 * P], in0=halves(c_pair[:, s, E:2 * E]),
                         in1=halves(t_pair[:, s, 0:E]), op=ALU.add,
@@ -254,14 +264,16 @@ def tile_attention_t_kernel(tc, x, Wk, bk, Wq, bq, Wv, bv, out_0, out_1, out_2):
         mx_pair(0)
         bias_table(0)
         bias_table(1)
+        times_cos(0)
         front_a(2)
         mx_pair(1)
         for i in range(PAIRS):
-            pool_adds_b1 = i < PAIRS - 1
-            back_first(i, pool_adds_b1)
+            if i + 1 < PAIRS:
+                times_cos(i + 1)
+            times_sin(i)
             if i + 2 < PAIRS:
                 front_b(i + 2)
-            back_second(i, pool_adds_b1)
+            back_second(i)
             if i + 3 < PAIRS:
                 front_a(i + 3)
             if i + 2 < PAIRS:

@@ -31,7 +31,7 @@ def tile_attention_t_kernel(tc, x, Wk, bk, Wq, bq, Wv, bv, out_0, out_1, out_2):
         gpool = ctx.enter_context(tc.tile_pool(name="gpool", bufs=2))
         cpool = ctx.enter_context(tc.tile_pool(name="cpool", bufs=4))
         tpool = ctx.enter_context(tc.tile_pool(name="tpool", bufs=4))
-        opool = ctx.enter_context(tc.tile_pool(name="opool", bufs=4))
+        opool = ctx.enter_context(tc.tile_pool(name="opool", bufs=8))
         ps_t = ctx.enter_context(tc.psum_pool(name="ps_t", bufs=2))
         ps_kq = ctx.enter_context(tc.psum_pool(name="ps_kq", bufs=4))
         ps_v = ctx.enter_context(tc.psum_pool(name="ps_v", bufs=2))

@@ -25,7 +25,6 @@ PAIRS = TOKENS // (2 * P)
 def tile_attention_t_kernel(tc, x, Wk, bk, Wq, bq, Wv, bv, out_0, out_1, out_2):
     nc = tc.nc
     with ExitStack() as ctx:
-        ctx.enter_context(tc.manual_schedule())
         const = ctx.enter_context(tc.tile_pool(name="const", bufs=1))
         xpool = ctx.enter_context(tc.tile_pool(name="xpool", bufs=1))
         gpool = ctx.enter_context(tc.tile_pool(name="gpool", bufs=2))

import math
from contextlib import ExitStack

import concourse.mybir as mybir
from concourse.masks import make_identity

FLOPS = 2 * 4096 * 1024 * 768

F32 = mybir.dt.float32
BF16 = mybir.dt.bfloat16
I32 = mybir.dt.int32
U32 = mybir.dt.uint32
U8 = mybir.dt.uint8
FP8X4 = mybir.dt.float8_e4m3fn_x4
ALU = mybir.AluOpType
ACT = mybir.ActivationFunctionType

P = 128
D = 1024
E = 256
TOKENS = 4096
PAIRS = TOKENS // (2 * P)


def tile_attention_t_kernel(tc, x, Wk, bk, Wq, bq, Wv, bv, out_0, out_1, out_2):
    nc = tc.nc
    with ExitStack() as ctx:
        const = ctx.enter_context(tc.tile_pool(name="const", bufs=1))
        xpool = ctx.enter_context(tc.tile_pool(name="xpool", bufs=1))
        gpool = ctx.enter_context(tc.tile_pool(name="gpool", bufs=2))
        cpool = ctx.enter_context(tc.tile_pool(name="cpool", bufs=4))
        tpool = ctx.enter_context(tc.tile_pool(name="tpool", bufs=4))
        opool = ctx.enter_context(tc.tile_pool(name="opool", bufs=8))
        ps_t = ctx.enter_context(tc.psum_pool(name="ps_t", bufs=2))
        ps_kq = ctx.enter_context(tc.psum_pool(name="ps_kq", bufs=4))
        ps_v = ctx.enter_context(tc.psum_pool(name="ps_v", bufs=2))

        xv = x.flatten_outer_dims().rearrange("(i q s) d -> i q (s d)", q=P, s=2)
        outs = [
            o.flatten_outer_dims().rearrange("(i q s) e -> i q (s e)", q=P, s=2)
            for o in (out_0, out_1, out_2)
        ]

        bland = const.tile([P, 3 * E], BF16, name="bland")
        for n, b in enumerate((bk, bq, bv)):
            nc.sync.dma_start(out=bland[0:1, n * E:(n + 1) * E], in_=b.rearrange("(o e) -> o e", o=1))
        wraw = []
        for n in range(3):
            wraw.append(const.tile([P, 2 * D], BF16, name="wraw%d" % n))
        xs = []
        for i in range(PAIRS):
            xs.append(xpool.tile([P, 2 * D], BF16, name="xs%d" % i))
        nc.sync.dma_start(out=wraw[0][:], in_=Wk.rearrange("(j h) d -> j (h d)", h=2))
        nc.sync.dma_start(out=wraw[1][:], in_=Wq.rearrange("(j h) d -> j (h d)", h=2))
        nc.sync.dma_start(out=xs[0][:], in_=xv[0])
        nc.sync.dma_start(
            out=wraw[2][:].rearrange("j (h d) -> j h d", h=2),
            in_=Wv.rearrange("(h j) d -> j h d", h=2),
        )
        for i in range(1, PAIRS):
            nc.sync.dma_start(out=xs[i][:], in_=xv[i])

        brow = const.tile([P, 3 * E], BF16, name="brow")
        ones = const.tile([P, P], BF16, name="ones")
        nc.vector.memset(brow[:], 0.0)
        nc.vector.memset(ones[:], 1.0)
        pos_i = const.tile([P, 2], I32, name="pos_i")
        nc.gpsimd.iota(pos_i[:], pattern=[[1, 2]], base=0, channel_multiplier=2)
        ident = const.tile([P, P], F32, name="ident")
        make_identity(nc, ident[:])

        pos_m = const.tile([P, 2], I32, name="pos_m")
        nc.vector.tensor_single_scalar(out=pos_m[:], in_=pos_i[:], scalar=127, op=ALU.bitwise_and)
        pos_f = const.tile([P, 2], F32, name="pos_f")
        nc.vector.tensor_copy(out=pos_f[:], in_=pos_m[:])
        decay = const.tile([P, 2], F32, name="decay")
        nc.scalar.activation(out=decay[:], in_=pos_f[:], func=ACT.Exp, scale=-math.log(10000.0) / 128.0)
        theta = const.tile([P, 2], F32, name="theta")
        nc.vector.tensor_tensor(out=theta[:], in0=pos_f[:], in1=decay[:], op=ALU.mult)
        s_half = const.tile([P, 2], F32, name="s_half")
        s_quart = const.tile([P, 2], F32, name="s_quart")
        nc.scalar.activation(out=s_half[:], in_=theta[:], func=ACT.Sin, scale=0.5)
        nc.scalar.activation(out=s_quart[:], in_=theta[:], func=ACT.Sin, scale=0.25)

        nc.vector.tensor_copy(out=brow[0:1, :], in_=bland[0:1, :])
        bkq_ps = ps_kq.tile([P, 2 * E], F32, name="bkq_ps", tag="kq")
        bv_ps = ps_v.tile([P, 2, E], F32, name="bv_ps", tag="v")
        nc.tensor.matmul(out=bkq_ps[:], lhsT=ones[:], rhs=brow[:, 0:2 * E], start=True, stop=True)
        nc.tensor.matmul(out=bv_ps[:, 0, :], lhsT=ones[:], rhs=brow[:, 2 * E:3 * E], start=True, stop=True)
        b_eo = const.tile([P, 2 * E], F32, name="b_eo")
        b_sw = const.tile([P, 2 * E], F32, name="b_sw")
        b_v = const.tile([P, E], F32, name="b_v")
        bkq_view = bkq_ps[:].rearrange("p (w j h) -> p h w j", w=2, h=2)
        nc.scalar.copy(out=b_eo[:].rearrange("p (h w j) -> p h w j", h=2, w=2), in_=bkq_view)
        nc.vector.tensor_copy(out=b_sw[:, 0:E].rearrange("p (w j) -> p w j", w=2), in_=bkq_view[:, 1])
        nc.vector.tensor_scalar(
            out=b_sw[:, E:2 * E].rearrange("p (w j) -> p w j", w=2), in0=bkq_view[:, 0],
            scalar1=-1.0, scalar2=None, op0=ALU.mult,
        )
        nc.scalar.copy(out=b_v[:], in_=bv_ps[:, 0, :])

        sq_q = const.tile([P, 2], F32, name="sq_q")
        c_half = const.tile([P, 2], F32, name="c_half")
        sin_t = const.tile([P, 2], F32, name="sin_t")
        sq_h = const.tile([P, 2], F32, name="sq_h")
        cos_t = const.tile([P, 2], F32, name="cos_t")
        nc.vector.tensor_tensor(out=sq_q[:], in0=s_quart[:], in1=s_quart[:], op=ALU.mult)
        nc.vector.tensor_tensor(out=sq_h[:], in0=s_half[:], in1=s_half[:], op=ALU.mult)
        nc.vector.tensor_scalar(out=c_half[:], in0=sq_q[:], scalar1=-2.0, scalar2=1.0, op0=ALU.mult, op1=ALU.add)
        nc.vector.tensor_scalar(out=cos_t[:], in0=sq_h[:], scalar1=-2.0, scalar2=1.0, op0=ALU.mult, op1=ALU.add)
        nc.vector.scalar_tensor_tensor(
            out=sin_t[:], in0=s_half[:], scalar=2.0, in1=c_half[:], op0=ALU.mult, op1=ALU.mult
        )

        wgrp = const.tile([P, 2 * 6 * 4 * P], BF16, name="wgrp", align_bytes=64)
        wcod = const.tile([P, 2, 6 * P], U32, name="wcod", align_bytes=64)
        wscl = const.tile([P, 2, 6 * P], U8, name="wscl", align_bytes=64)
        wgrp_w = wgrp[:].bitcast(F32).rearrange("p (g c r u) -> p g c r u", g=2, c=6, u=2)

        def transposes(words, pool, tag):
            tb = pool.tile([P, 4, P], F32, name="tb_" + tag, tag=tag)
            for c in range(4):
                nc.tensor.transpose(tb[:, c, :], words[:, c * P:(c + 1) * P], ident[:])
            return tb[:].rearrange("p (g u) q -> p g q u", u=2)

        def weight_tile(col, raw, half, on_vector):
            pool, tag = (ps_kq, "kq") if col < 4 else (ps_v, "v")
            src = transposes(raw[:].bitcast(F32)[:, half * (D // 2):(half + 1) * (D // 2)], pool, tag)
            if on_vector:
                nc.vector.tensor_copy(out=wgrp_w[:, :, col], in_=src)
            else:
                nc.scalar.copy(out=wgrp_w[:, :, col], in_=src)

        def weight_quant(lo, hi):
            for g in range(2):
                nc.vector.quantize_mx(
                    out=wcod[:, g, lo * P:hi * P].bitcast(FP8X4),
                    scales=wscl[:, g, lo * P:hi * P],
                    in_=wgrp[:, (g * 6 + lo) * 4 * P:(g * 6 + hi) * 4 * P],
                )

        grouped = {}
        codes = {}
        banks = {}
        parts = {}
        cosines = {}

        def front_a(i):
            grp = gpool.tile([P, 2 * D], BF16, name="grp", tag="grp", align_bytes=64)
            grp_w = grp[:].bitcast(F32).rearrange("p (s g q u) -> p s g q u", s=2, g=2, u=2)
            words = xs[i][:].bitcast(F32)
            for s in range(2):
                src = transposes(words[:, s * (D // 2):(s + 1) * (D // 2)], ps_t, "t")
                nc.scalar.copy(out=grp_w[:, s], in_=src)
            grouped[i] = grp

        def front_b(i):
            cod = cpool.tile([P, 4 * P], U32, name="cod", tag="cod", align_bytes=64)
            scl = cpool.tile([P, 4 * P], U8, name="scl", tag="scl", align_bytes=64)
            nc.vector.quantize_mx(out=cod[:].bitcast(FP8X4), scales=scl[:], in_=grouped[i][:])
            codes[i] = (cod, scl)

        bias_x = const.tile([P, 2, 2 * E], F32, name="bias_x")

        def bias_table(s):
            tmp = tpool.tile([P, 2 * E], F32, name="tmp", tag="tmp", bufs=2)
            nc.scalar.activation(out=tmp[:], in_=b_sw[:], func=ACT.Copy, scale=cos_t[:, s:s + 1])
            nc.vector.scalar_tensor_tensor(
                out=bias_x[:, s, :], in0=b_eo[:], scalar=sin_t[:, s:s + 1], in1=tmp[:],
                op0=ALU.mult, op1=ALU.add,
            )

        def mx_pair(i):
            cod, scl = codes[i]
            kq = []
            for s in range(2):
                acc = ps_kq.tile([P, 2 * E], F32, name="kq", tag="kq")
                for g in range(2):
                    cols = slice((2 * s + g) * P, (2 * s + g + 1) * P)
                    nc.tensor.matmul_mx(
                        out=acc[:], lhsT=cod[:, cols].bitcast(FP8X4), lhsT_scale=scl[:, cols],
                        rhs=wcod[:, g, 0:4 * P].bitcast(FP8X4), rhs_scale=wscl[:, g, 0:4 * P],
                        start=(g == 0), stop=(g == 1),
                    )
                kq.append(acc)
            vb = ps_v.tile([P, 2, E], F32, name="vb", tag="v")
            for s in range(2):
                for g in range(2):
                    cols = slice((2 * s + g) * P, (2 * s + g + 1) * P)
                    nc.tensor.matmul_mx(
                        out=vb[:, s, :], lhsT=cod[:, cols].bitcast(FP8X4), lhsT_scale=scl[:, cols],
                        rhs=wcod[:, g, 4 * P:6 * P].bitcast(FP8X4), rhs_scale=wscl[:, g, 4 * P:6 * P],
                        start=(g == 0), stop=(g == 1),
                    )
            banks[i] = (kq, vb)

        def halves(ap):
            return ap.rearrange("p (w j) -> p w j", w=2)

        def pool_adds_b1(i):
            return 0 < i < PAIRS - 1

        def times_cos(i):
            kq = banks[i][0]
            c_pair = tpool.tile([P, 2, 2 * E], F32, name="c_pair", tag="c_pair")
            for s in range(2):
                width = 2 * E if (s == 1 and pool_adds_b1(i)) else E
                nc.scalar.activation(
                    out=c_pair[:, s, 0:width], in_=kq[s][:, 0:width], func=ACT.Copy, scale=cos_t[:, s:s + 1]
                )
            cosines[i] = c_pair

        def times_sin(i):
            kq = banks[i][0]
            t_pair = tpool.tile([P, 2, 2 * E], F32, name="t_pair", tag="t_pair")
            for s in range(2):
                nc.vector.scalar_tensor_tensor(
                    out=t_pair[:, s, :], in0=kq[s][:], scalar=sin_t[:, s:s + 1], in1=bias_x[:, s, :],
                    op0=ALU.mult, op1=ALU.add,
                )
            parts[i] = t_pair

        def back_second(i):
            kq, vb = banks[i]
            t_pair = parts[i]
            c_pair = cosines[i]
            o = opool.tile([P, 3, 2, E], F32, name="stage", tag="stage")
            nc.gpsimd.tensor_tensor(
                out=o[:, 0:2, :, 0:P],
                in0=c_pair[:, :, 0:E].rearrange("p s (w j) -> p w s j", w=2),
                in1=t_pair[:, :, E:2 * E].rearrange("p s (w j) -> p w s j", w=2),
                op=ALU.subtract,
            )
            for s in range(2):
                if s == 1 and pool_adds_b1(i):
                    nc.gpsimd.tensor_tensor(
                        out=o[:, 0:2, s, P:2 * P], in0=halves(c_pair[:, s, E:2 * E]),
                        in1=halves(t_pair[:, s, 0:E]), op=ALU.add,
                    )
                else:
                    nc.vector.scalar_tensor_tensor(
                        out=o[:, 0:2, s, P:2 * P], in0=halves(kq[s][:, E:2 * E]), scalar=cos_t[:, s:s + 1],
                        in1=halves(t_pair[:, s, 0:E]), op0=ALU.mult, op1=ALU.add,
                    )
            nc.vector.tensor_tensor(
                out=o[:, 2, :, :], in0=vb[:], in1=b_v[:].unsqueeze(1).to_broadcast([P, 2, E]), op=ALU.add
            )
            for n in (2, 0, 1):
                nc.sync.dma_start(out=outs[n][i], in_=o[:, n, :, :].rearrange("p s e -> p (s e)"))

        weight_tile(0, wraw[0], 0, False)
        weight_tile(2, wraw[0], 1, True)
        weight_tile(1, wraw[1], 0, False)
        weight_tile(3, wraw[1], 1, True)
        weight_quant(0, 4)
        front_a(0)
        front_b(0)
        weight_tile(4, wraw[2], 0, False)
        weight_tile(5, wraw[2], 1, False)
        weight_quant(4, 6)
        front_a(1)
        front_b(1)
        mx_pair(0)
        bias_table(0)
        bias_table(1)
        times_cos(0)
        front_a(2)
        mx_pair(1)
        for i in range(PAIRS):
            if i + 1 < PAIRS:
                times_cos(i + 1)
            times_sin(i)
            if i + 2 < PAIRS:
                front_b(i + 2)
            back_second(i)
            if i + 3 < PAIRS:
                front_a(i + 3)
            if i + 2 < PAIRS:
                mx_pair(i + 2)
